import numpy as np
import ml_dtypes


def mxq(x, axis, fmt="e4m3"):
    dtype, down = {"e4m3": (ml_dtypes.float8_e4m3fn, 7), "e5m2": (ml_dtypes.float8_e5m2, 14)}[fmt]
    v = np.moveaxis(np.asarray(x, np.float32).astype(ml_dtypes.bfloat16).astype(np.float64), axis, -1)
    blocks = v.reshape(v.shape[:-1] + (-1, 32))
    amax = np.abs(blocks).max(-1, keepdims=True)
    byte = np.maximum(np.where(amax > 0, np.frexp(amax)[1] - 1 + 127, 0) - down, 1)
    scale = np.exp2(byte - 127.0)
    codes = (blocks / scale).astype(np.float32).astype(dtype).astype(np.float64)
    return np.moveaxis((codes * scale).reshape(v.shape), -1, axis)


WIDE = False


def mx_kscale(k):
    if not WIDE:
        return np.ones(k)
    levels = np.array([10, -10, 5, -5, 0])
    if k % 512:
        return np.exp2(np.random.permutation(np.resize(levels, k // 32))).repeat(32)
    a = np.empty((k // 512, 16))
    for p in range(k // 512):
        a[p, :8] = np.random.permutation(np.resize(levels, 8))
        for g in range(8):
            far = levels[np.abs(levels - a[p, g]) >= 10]
            a[p, g + 8] = far[np.random.randint(len(far))]
    return np.exp2(a.ravel()).repeat(32)


BF16 = ml_dtypes.bfloat16


def bf(x):
    return np.asarray(x, np.float32).astype(BF16)


def f64(x):
    return np.asarray(x).astype(np.float64)


B, L, C, KS, NL, BH, R = 1, 128, 512, 4, 24, 8, 4
OUT = 2 * BH * NL


def setup_inputs():
    s, t = mx_kscale(C), mx_kscale(C)
    return {"local_features": bf(np.random.standard_normal((B, L, C)) * s),
            "wt": bf(np.random.standard_normal((C, C, KS)) / np.sqrt(C) / s[:, None, None] * t[None, :, None]),
            "bt": bf(np.random.standard_normal(C) * 0.5 * t),
            "w1": bf(np.random.standard_normal((OUT, C)) / np.sqrt(C) / t[None, :]),
            "b1": bf(np.random.standard_normal(OUT) * 0.5)}


def reference(local_features, wt, bt, w1, b1):
    xq = mxq(f64(local_features), 2, "e4m3")
    wq = mxq(f64(wt), 0, "e4m3")
    up = xq @ wq.reshape(C, C * KS)
    up = up.reshape(B, L, C, KS).transpose(0, 2, 1, 3).reshape(B, C, L * KS) + f64(bt)[None, :, None]
    y = (mxq(f64(w1), 1, "e4m3") @ mxq(up, 1, "e4m3")) + f64(b1)[None, :, None]
    y = np.tile(y, (1, 1, R))
    y = y.reshape(B, NL, 2 * BH, L * KS * R)
    return np.ascontiguousarray(y.transpose(2, 0, 1, 3))

@@ -1,0 +1,221 @@
+from contextlib import ExitStack
+
+import concourse.mybir as mybir
+from concourse.masks import make_identity
+
+BF16 = mybir.dt.bfloat16
+F32 = mybir.dt.float32
+U32 = mybir.dt.uint32
+U8 = mybir.dt.uint8
+FP8X4 = mybir.dt.float8_e4m3fn_x4
+IDENTITY = mybir.ActivationFunctionType.Identity
+
+P = 128
+PACK = 4
+L = 128
+C = 512
+TAPS = 4
+T = L * TAPS
+OUT = 384
+REPEAT = 4
+HEADS = 16
+O_TILES = C // P
+Y_TILES = OUT // P
+BIAS_BLOCKS = O_TILES + Y_TILES
+HALVES = 2
+HALF_TAPS = TAPS // HALVES
+HALF_T = T // HALVES
+UNITS = O_TILES * HALVES
+
+WT_VECTOR_COLS = 88
+UP_VECTOR_STEPS = 192
+CHUNKS_BEFORE_W1 = 2
+
+FLOPS = 2 * L * C * C * TAPS + 2 * OUT * C * T
+
+
+def tile_conditionalfeaturesupsample_s_kernel(tc, local_features, wt, bt, w1, b1, out):
+    nc = tc.nc
+    with ExitStack() as ctx:
+        ctx.enter_context(tc.manual_schedule())
+        const = ctx.enter_context(tc.tile_pool(name="const", bufs=1))
+        units = ctx.enter_context(tc.tile_pool(name="units", bufs=UNITS))
+        results = ctx.enter_context(tc.tile_pool(name="results", bufs=Y_TILES))
+        psum_t = ctx.enter_context(tc.psum_pool(name="psum_t", bufs=Y_TILES))
+        psum_up = ctx.enter_context(tc.psum_pool(name="psum_up", bufs=2))
+        psum_y = ctx.enter_context(tc.psum_pool(name="psum_y", bufs=Y_TILES))
+
+        x_sb = const.tile([P, C], BF16)
+        nc.sync.dma_start(out=x_sb[:], in_=local_features[0])
+        bias_rows = const.tile([P, BIAS_BLOCKS * P], BF16)
+        nc.vector.memset(bias_rows[:], 0.0)
+        nc.sync.dma_start(out=bias_rows[0:1, 0:C], in_=bt.rearrange("(a c) -> a c", a=1))
+        b1_row = const.tile([1, OUT], BF16)
+        nc.sync.dma_start(out=b1_row[:], in_=b1.rearrange("(a c) -> a c", a=1))
+        wt_rows = wt.rearrange("(p t) o k -> p t (o k)", p=P)
+        wt_raw = const.tile([P, PACK, C * TAPS], BF16)
+        chunk_cols = P * TAPS
+        w1_sb = const.tile([P, Y_TILES, C], BF16)
+        for h in range(O_TILES):
+            if h == CHUNKS_BEFORE_W1:
+                nc.sync.dma_start(out=w1_sb[:], in_=w1.rearrange("(a r) o -> r a o", r=P))
+            cols = slice(h * chunk_cols, (h + 1) * chunk_cols)
+            nc.sync.dma_start(out=wt_raw[:, :, cols], in_=wt_rows[:, :, cols])
+
+        ident = const.tile([P, P], BF16)
+        make_identity(nc, ident[:])
+
+        x_ps = psum_t.tile([P, PACK, L], BF16, tag="transposed")
+        for t in range(PACK):
+            nc.tensor.transpose(x_ps[:, t, :], x_sb[:, t:C:PACK], ident[:])
+        x_grouped = const.tile([P, L, PACK], BF16, align_bytes=64)
+        nc.vector.tensor_copy(out=x_grouped[:], in_=x_ps[:].rearrange("p t l -> p l t"))
+        x_codes = const.tile([P, L], U32, align_bytes=64)
+        x_scales = const.tile([P, L], U8, align_bytes=64)
+        nc.vector.quantize_mx(
+            out=x_codes[:].bitcast(FP8X4),
+            scales=x_scales[:],
+            in_=x_grouped[:].rearrange("p l t -> p (l t)"),
+        )
+
+        nc.vector.tensor_copy(
+            out=bias_rows[0:1, C : C + OUT].rearrange("a (j n) -> a j n", j=HEADS),
+            in_=b1_row[:].rearrange("a (n j) -> a j n", j=HEADS),
+        )
+        bias_ps = psum_t.tile([P, BIAS_BLOCKS, P], BF16, tag="transposed")
+        for blk in range(BIAS_BLOCKS):
+            cols = slice(blk, C, O_TILES) if blk < O_TILES else slice(blk * P, (blk + 1) * P)
+            nc.tensor.transpose(bias_ps[:, blk, :], bias_rows[:, cols], ident[:])
+        bias_cols = const.tile([P, BIAS_BLOCKS], F32)
+
+        w1_codes = const.tile([P, OUT], U32, align_bytes=64)
+        w1_scales = const.tile([P, OUT], U8, align_bytes=64)
+
+        w1_grouped = const.tile([P, OUT, PACK], BF16, align_bytes=64)
+        w1_ps_tiles = []
+
+        def transpose_w1():
+            for a in range(Y_TILES):
+                w1_ps = psum_t.tile([P, PACK, P], BF16, tag="transposed")
+                for t in range(PACK):
+                    nc.tensor.transpose(w1_ps[:, t, :], w1_sb[:, a, t:C:PACK], ident[:])
+                w1_ps_tiles.append(w1_ps)
+
+        def regroup_w1():
+            w1_by_head = w1_grouped[:].rearrange("p (j n) t -> p j n t", j=HEADS)
+            layers_per_tile = P // HEADS
+            for a in range(Y_TILES):
+                nc.scalar.copy(
+                    out=w1_by_head[:, :, a * layers_per_tile : (a + 1) * layers_per_tile, :],
+                    in_=w1_ps_tiles[a][:].rearrange("p t (n j) -> p j n t", j=HEADS),
+                )
+
+        def quantise_w1():
+            for a in range(Y_TILES):
+                rows = slice(a * P, (a + 1) * P)
+                nc.vector.quantize_mx(
+                    out=w1_codes[:, rows].bitcast(FP8X4),
+                    scales=w1_scales[:, rows],
+                    in_=w1_grouped[:, rows, :].rearrange("p q t -> p (q t)"),
+                )
+
+        def regroup_wt(u):
+            h, half = divmod(u, HALVES)
+            taps = slice(half * HALF_TAPS, (half + 1) * HALF_TAPS)
+            wt_grouped = units.tile([P, HALF_TAPS, P, PACK], BF16, align_bytes=64)
+            src = wt_raw[:].rearrange("p t (m h k) -> p h m t k", h=O_TILES, k=TAPS)[:, h, :, :, taps]
+            dst = wt_grouped[:].rearrange("p k m t -> p m t k")
+            nc.vector.tensor_copy(out=dst[:, 0:WT_VECTOR_COLS], in_=src[:, 0:WT_VECTOR_COLS])
+            nc.scalar.copy(out=dst[:, WT_VECTOR_COLS:P], in_=src[:, WT_VECTOR_COLS:P])
+            return wt_grouped
+
+        def quantise_and_multiply(wt_grouped):
+            wt_codes = units.tile([P, HALF_TAPS, P], U32, align_bytes=64)
+            wt_scales = units.tile([P, HALF_TAPS, P], U8, align_bytes=64)
+            nc.vector.quantize_mx(
+                out=wt_codes[:].rearrange("p k m -> p (k m)").bitcast(FP8X4),
+                scales=wt_scales[:].rearrange("p k m -> p (k m)"),
+                in_=wt_grouped[:].rearrange("p k m t -> p (k m t)"),
+            )
+            up_ps = psum_up.tile([P, HALF_TAPS, L], F32)
+            for k in range(HALF_TAPS):
+                nc.tensor.matmul_mx(
+                    out=up_ps[:, k, :],
+                    lhsT=wt_codes[:, k, :].bitcast(FP8X4),
+                    lhsT_scale=wt_scales[:, k, :],
+                    rhs=x_codes[:].bitcast(FP8X4),
+                    rhs_scale=x_scales[:],
+                    start=True,
+                    stop=True,
+                )
+            return up_ps
+
+        up_planes = const.tile([P, HALVES, O_TILES, HALF_T], BF16)
+
+        def add_bt(u, up_ps):
+            h, half = divmod(u, HALVES)
+            nc.scalar.activation(
+                out=up_planes[:, half, h, :],
+                in_=up_ps[:].rearrange("p k l -> p (k l)"),
+                func=IDENTITY,
+                bias=bias_cols[:, h : h + 1],
+            )
+
+        grouped_tiles = [regroup_wt(0)]
+        nc.scalar.copy(out=bias_cols[:], in_=bias_ps[:, :, 0])
+        up_ps_tiles = []
+        for u in range(UNITS):
+            if u + 1 < UNITS:
+                grouped_tiles.append(regroup_wt(u + 1))
+            up_ps_tiles.append(quantise_and_multiply(grouped_tiles[u]))
+            if u >= 1:
+                add_bt(u - 1, up_ps_tiles[u - 1])
+            if u + 1 == CHUNKS_BEFORE_W1 * HALVES:
+                transpose_w1()
+            if u == CHUNKS_BEFORE_W1 * HALVES:
+                regroup_w1()
+        quantise_w1()
+
+        up_grouped = const.tile([P, HALVES, HALF_T, PACK], BF16, align_bytes=64)
+        up_codes = const.tile([P, T], U32, align_bytes=64)
+        up_scales = const.tile([P, T], U8, align_bytes=64)
+        src = up_planes[:].rearrange("p f h (c i) -> p f c h i", i=4)
+        dst = up_grouped[:].rearrange("p f (c i) h -> p f c h i", i=4)
+        split = UP_VECTOR_STEPS // 4
+        nc.vector.tensor_copy(out=dst[:, 0], in_=src[:, 0])
+        add_bt(UNITS - 1, up_ps_tiles[UNITS - 1])
+        nc.vector.tensor_copy(out=dst[:, 1, 0:split], in_=src[:, 1, 0:split])
+        nc.scalar.copy(out=dst[:, 1, split : HALF_T // 4], in_=src[:, 1, split : HALF_T // 4])
+        for half in range(HALVES):
+            steps = slice(half * HALF_T, (half + 1) * HALF_T)
+            nc.vector.quantize_mx(
+                out=up_codes[:, steps].bitcast(FP8X4),
+                scales=up_scales[:, steps],
+                in_=up_grouped[:, half].rearrange("p s h -> p (s h)"),
+            )
+
+        out_rows = out.rearrange("j b n s -> (j b n) s")
+        for a in range(Y_TILES):
+            rows = slice(a * P, (a + 1) * P)
+            y_ps = psum_y.tile([P, T], F32)
+            for half in range(HALVES):
+                steps = slice(half * HALF_T, (half + 1) * HALF_T)
+                nc.tensor.matmul_mx(
+                    out=y_ps[:, steps],
+                    lhsT=w1_codes[:, rows].bitcast(FP8X4),
+                    lhsT_scale=w1_scales[:, rows],
+                    rhs=up_codes[:, steps].bitcast(FP8X4),
+                    rhs_scale=up_scales[:, steps],
+                    start=True,
+                    stop=True,
+                )
+            y_sb = results.tile([P, T], F32)
+            y_in_time = y_sb[:].rearrange("p (l k) -> p l k", k=TAPS)
+            y_by_tap = y_ps[:].rearrange("p (k l) -> p l k", k=TAPS)
+            b1_col = bias_cols[:, O_TILES + a : O_TILES + a + 1]
+            if a % 2 == 0:
+                nc.vector.tensor_scalar_add(out=y_in_time, in0=y_by_tap, scalar1=b1_col)
+            else:
+                nc.scalar.activation(out=y_in_time, in_=y_by_tap, func=IDENTITY, bias=b1_col)
+            for r in range(REPEAT):
+                nc.sync.dma_start(out=out_rows[rows, r * T : (r + 1) * T], in_=y_sb[:])

@@ -9,9 +9,11 @@ U32 = mybir.dt.uint32
 U8 = mybir.dt.uint8
 FP8X4 = mybir.dt.float8_e4m3fn_x4
 IDENTITY = mybir.ActivationFunctionType.Identity
+ADD = mybir.AluOpType.add
 
 P = 128
 PACK = 4
+PAIRS = 2
 L = 128
 C = 512
 TAPS = 4
@@ -19,17 +21,14 @@ T = L * TAPS
 OUT = 384
 REPEAT = 4
 HEADS = 16
-O_TILES = C // P
+LAYERS = OUT // HEADS
 Y_TILES = OUT // P
-BIAS_BLOCKS = O_TILES + Y_TILES
+CHUNKS = 4
+CHUNK_O = C // CHUNKS
+CHUNK_M = CHUNK_O // PACK
 HALVES = 2
-HALF_TAPS = TAPS // HALVES
+HALF_L = L // HALVES
 HALF_T = T // HALVES
-UNITS = O_TILES * HALVES
-
-WT_VECTOR_COLS = 88
-UP_VECTOR_STEPS = 192
-CHUNKS_BEFORE_W1 = 2
 
 FLOPS = 2 * L * C * C * TAPS + 2 * OUT * C * T
 
@@ -39,183 +38,203 @@ def tile_conditionalfeaturesupsample_s_kernel(tc, local_features, wt, bt, w1, b1
     with ExitStack() as ctx:
         ctx.enter_context(tc.manual_schedule())
         const = ctx.enter_context(tc.tile_pool(name="const", bufs=1))
-        units = ctx.enter_context(tc.tile_pool(name="units", bufs=UNITS))
-        results = ctx.enter_context(tc.tile_pool(name="results", bufs=Y_TILES))
-        psum_t = ctx.enter_context(tc.psum_pool(name="psum_t", bufs=Y_TILES))
-        psum_up = ctx.enter_context(tc.psum_pool(name="psum_up", bufs=2))
-        psum_y = ctx.enter_context(tc.psum_pool(name="psum_y", bufs=Y_TILES))
+        chunks = ctx.enter_context(tc.tile_pool(name="chunks", bufs=CHUNKS))
+        results = ctx.enter_context(tc.tile_pool(name="results", bufs=Y_TILES * HALVES))
+        banks = ctx.enter_context(tc.psum_pool(name="banks", bufs=8))
 
         x_sb = const.tile([P, C], BF16)
         nc.sync.dma_start(out=x_sb[:], in_=local_features[0])
-        bias_rows = const.tile([P, BIAS_BLOCKS * P], BF16)
-        nc.vector.memset(bias_rows[:], 0.0)
-        nc.sync.dma_start(out=bias_rows[0:1, 0:C], in_=bt.rearrange("(a c) -> a c", a=1))
         b1_row = const.tile([1, OUT], BF16)
-        nc.sync.dma_start(out=b1_row[:], in_=b1.rearrange("(a c) -> a c", a=1))
+        nc.scalar.dma_start(out=b1_row[:], in_=b1.rearrange("(a c) -> a c", a=1))
+        bt_cols = const.tile([P, PACK], BF16)
+        nc.scalar.dma_start(out=bt_cols[:], in_=bt.rearrange("(p t) -> p t", t=PACK))
         wt_rows = wt.rearrange("(p t) o k -> p t (o k)", p=P)
-        wt_raw = const.tile([P, PACK, C * TAPS], BF16)
-        chunk_cols = P * TAPS
+        wt_raw_tiles = []
+        for c in range(CHUNKS):
+            wt_raw = chunks.tile([P, PACK, CHUNK_O * TAPS], BF16)
+            nc.sync.dma_start(
+                out=wt_raw[:], in_=wt_rows[:, :, c * CHUNK_O * TAPS : (c + 1) * CHUNK_O * TAPS]
+            )
+            wt_raw_tiles.append(wt_raw)
         w1_sb = const.tile([P, Y_TILES, C], BF16)
-        for h in range(O_TILES):
-            if h == CHUNKS_BEFORE_W1:
-                nc.sync.dma_start(out=w1_sb[:], in_=w1.rearrange("(a r) o -> r a o", r=P))
-            cols = slice(h * chunk_cols, (h + 1) * chunk_cols)
-            nc.sync.dma_start(out=wt_raw[:, :, cols], in_=wt_rows[:, :, cols])
+        nc.sync.dma_start(out=w1_sb[:], in_=w1.rearrange("(a r) o -> r a o", r=P))
 
-        ident = const.tile([P, P], BF16)
+        warm = const.tile([P, 2], F32)
+        nc.vector.memset(warm[:, 0:1], 0.0)
+        nc.scalar.activation(out=warm[:, 1:2], in_=warm[:, 0:1], func=IDENTITY)
+        ident = const.tile([P, P], F32)
         make_identity(nc, ident[:])
+        bias_rows = const.tile([P, OUT], F32)
+        nc.gpsimd.memset(bias_rows[:], 0.0)
 
-        x_ps = psum_t.tile([P, PACK, L], BF16, tag="transposed")
-        for t in range(PACK):
-            nc.tensor.transpose(x_ps[:, t, :], x_sb[:, t:C:PACK], ident[:])
-        x_grouped = const.tile([P, L, PACK], BF16, align_bytes=64)
-        nc.vector.tensor_copy(out=x_grouped[:], in_=x_ps[:].rearrange("p t l -> p l t"))
+        x_words = x_sb[:].bitcast(F32)
+        x_ps = banks.tile([P, PAIRS, L], F32, tag="bank")
+        for u in range(PAIRS):
+            nc.tensor.transpose(x_ps[:, u, :], x_words[:, u : C // 2 : PAIRS], ident[:])
+        x_grouped = const.tile([P, L * PACK], BF16, align_bytes=64)
+        nc.scalar.copy(
+            out=x_grouped[:].bitcast(F32).rearrange("p (l u) -> p l u", u=PAIRS),
+            in_=x_ps[:].rearrange("p u l -> p l u"),
+        )
         x_codes = const.tile([P, L], U32, align_bytes=64)
         x_scales = const.tile([P, L], U8, align_bytes=64)
-        nc.vector.quantize_mx(
-            out=x_codes[:].bitcast(FP8X4),
-            scales=x_scales[:],
-            in_=x_grouped[:].rearrange("p l t -> p (l t)"),
-        )
 
         nc.vector.tensor_copy(
-            out=bias_rows[0:1, C : C + OUT].rearrange("a (j n) -> a j n", j=HEADS),
+            out=bias_rows[0:1, :].rearrange("a (j n) -> a j n", j=HEADS),
             in_=b1_row[:].rearrange("a (n j) -> a j n", j=HEADS),
         )
-        bias_ps = psum_t.tile([P, BIAS_BLOCKS, P], BF16, tag="transposed")
-        for blk in range(BIAS_BLOCKS):
-            cols = slice(blk, C, O_TILES) if blk < O_TILES else slice(blk * P, (blk + 1) * P)
-            nc.tensor.transpose(bias_ps[:, blk, :], bias_rows[:, cols], ident[:])
-        bias_cols = const.tile([P, BIAS_BLOCKS], F32)
+        nc.vector.quantize_mx(out=x_codes[:].bitcast(FP8X4), scales=x_scales[:], in_=x_grouped[:])
+        b1_ps = banks.tile([P, Y_TILES], F32, tag="bank")
+        for a in range(Y_TILES):
+            nc.tensor.matmul(
+                b1_ps[:, a : a + 1], lhsT=bias_rows[:, a * P : (a + 1) * P], rhs=ident[:, 0:1], start=True, stop=True
+            )
+        b1_cols = const.tile([P, Y_TILES], F32)
 
+        wt_grouped = const.tile([P, TAPS, PACK, P, PACK], BF16, align_bytes=64)
+        wt_by_channel = wt_grouped[:].rearrange("p k h m t -> p h m t k")
+
+        def regroup(copy, c, heads, taps):
+            cols = slice(c * CHUNK_M, (c + 1) * CHUNK_M)
+            src = wt_raw_tiles[c][:].rearrange("p t (m h k) -> p h m t k", h=PACK, k=TAPS)
+            copy(out=wt_by_channel[:, heads, cols, :, taps], in_=src[:, heads, :, :, taps])
+
+        for c in range(CHUNKS):
+            regroup(nc.vector.tensor_copy, c, slice(0, PACK), slice(0, 2))
+            regroup(nc.scalar.copy, c, slice(1, PACK), slice(2, TAPS))
+            regroup(nc.vector.tensor_copy, c, slice(0, 1), slice(2, TAPS))
+
+        w1_words = w1_sb[:].rearrange("r a o -> r (a o)").bitcast(F32)
+        w1_grouped = const.tile([P, OUT * PACK], BF16, align_bytes=64)
+        w1_by_head = w1_grouped[:].bitcast(F32).rearrange("p (j n u) -> p j n u", j=HEADS, u=PAIRS)
+        layers_per_tile = P // HEADS
+        w1_ps_tiles = []
+        for a in range(Y_TILES):
+            w1_ps = banks.tile([P, PAIRS, P], F32, tag="bank")
+            first = a * (C // 2)
+            for u in range(PAIRS):
+                nc.tensor.transpose(w1_ps[:, u, :], w1_words[:, first + u : first + C // 2 : PAIRS], ident[:])
+            w1_ps_tiles.append(w1_ps)
+        for a in range(Y_TILES):
+            nc.scalar.copy(
+                out=w1_by_head[:, :, a * layers_per_tile : (a + 1) * layers_per_tile, :],
+                in_=w1_ps_tiles[a][:].rearrange("p u (n j) -> p j n u", j=HEADS),
+            )
+        nc.scalar.copy(out=b1_cols[:], in_=b1_ps[:])
         w1_codes = const.tile([P, OUT], U32, align_bytes=64)
         w1_scales = const.tile([P, OUT], U8, align_bytes=64)
 
-        w1_grouped = const.tile([P, OUT, PACK], BF16, align_bytes=64)
-        w1_ps_tiles = []
-
-        def transpose_w1():
-            for a in range(Y_TILES):
-                w1_ps = psum_t.tile([P, PACK, P], BF16, tag="transposed")
-                for t in range(PACK):
-                    nc.tensor.transpose(w1_ps[:, t, :], w1_sb[:, a, t:C:PACK], ident[:])
-                w1_ps_tiles.append(w1_ps)
-
-        def regroup_w1():
-            w1_by_head = w1_grouped[:].rearrange("p (j n) t -> p j n t", j=HEADS)
-            layers_per_tile = P // HEADS
-            for a in range(Y_TILES):
-                nc.scalar.copy(
-                    out=w1_by_head[:, :, a * layers_per_tile : (a + 1) * layers_per_tile, :],
-                    in_=w1_ps_tiles[a][:].rearrange("p t (n j) -> p j n t", j=HEADS),
-                )
-
-        def quantise_w1():
-            for a in range(Y_TILES):
-                rows = slice(a * P, (a + 1) * P)
-                nc.vector.quantize_mx(
-                    out=w1_codes[:, rows].bitcast(FP8X4),
-                    scales=w1_scales[:, rows],
-                    in_=w1_grouped[:, rows, :].rearrange("p q t -> p (q t)"),
-                )
-
-        def regroup_wt(u):
-            h, half = divmod(u, HALVES)
-            taps = slice(half * HALF_TAPS, (half + 1) * HALF_TAPS)
-            wt_grouped = units.tile([P, HALF_TAPS, P, PACK], BF16, align_bytes=64)
-            src = wt_raw[:].rearrange("p t (m h k) -> p h m t k", h=O_TILES, k=TAPS)[:, h, :, :, taps]
-            dst = wt_grouped[:].rearrange("p k m t -> p m t k")
-            nc.vector.tensor_copy(out=dst[:, 0:WT_VECTOR_COLS], in_=src[:, 0:WT_VECTOR_COLS])
-            nc.scalar.copy(out=dst[:, WT_VECTOR_COLS:P], in_=src[:, WT_VECTOR_COLS:P])
-            return wt_grouped
-
-        def quantise_and_multiply(wt_grouped):
-            wt_codes = units.tile([P, HALF_TAPS, P], U32, align_bytes=64)
-            wt_scales = units.tile([P, HALF_TAPS, P], U8, align_bytes=64)
+        def quantise_w1(a):
+            rows = slice(a * P, (a + 1) * P)
             nc.vector.quantize_mx(
-                out=wt_codes[:].rearrange("p k m -> p (k m)").bitcast(FP8X4),
-                scales=wt_scales[:].rearrange("p k m -> p (k m)"),
-                in_=wt_grouped[:].rearrange("p k m t -> p (k m t)"),
+                out=w1_codes[:, rows].bitcast(FP8X4),
+                scales=w1_scales[:, rows],
+                in_=w1_grouped[:, a * P * PACK : (a + 1) * P * PACK],
             )
-            up_ps = psum_up.tile([P, HALF_TAPS, L], F32)
-            for k in range(HALF_TAPS):
+
+        wt_codes = const.tile([P, TAPS, C], U32, align_bytes=64)
+        wt_scales = const.tile([P, TAPS, C], U8, align_bytes=64)
+        up_ps_tiles = []
+
+        def quantise_and_multiply(k, up_ps, heads):
+            cols = slice(heads[0] * P, (heads[-1] + 1) * P)
+            nc.vector.quantize_mx(
+                out=wt_codes[:, k, cols].bitcast(FP8X4),
+                scales=wt_scales[:, k, cols],
+                in_=wt_grouped[:, k, heads[0] : heads[-1] + 1].rearrange("p h m t -> p (h m t)"),
+            )
+            for h in heads:
+                cols = slice(h * P, (h + 1) * P)
                 nc.tensor.matmul_mx(
-                    out=up_ps[:, k, :],
-                    lhsT=wt_codes[:, k, :].bitcast(FP8X4),
-                    lhsT_scale=wt_scales[:, k, :],
+                    out=up_ps[:, h, :],
+                    lhsT=wt_codes[:, k, cols].bitcast(FP8X4),
+                    lhsT_scale=wt_scales[:, k, cols],
                     rhs=x_codes[:].bitcast(FP8X4),
                     rhs_scale=x_scales[:],
                     start=True,
                     stop=True,
                 )
-            return up_ps
 
-        up_planes = const.tile([P, HALVES, O_TILES, HALF_T], BF16)
+        for k in range(TAPS):
+            up_ps = banks.tile([P, PACK, L], F32, tag="bank")
+            if k < TAPS - 1:
+                quantise_and_multiply(k, up_ps, range(PACK))
+            else:
+                quantise_and_multiply(k, up_ps, range(PACK // 2))
+                quantise_and_multiply(k, up_ps, range(PACK // 2, PACK))
+            up_ps_tiles.append(up_ps)
 
-        def add_bt(u, up_ps):
-            h, half = divmod(u, HALVES)
-            nc.scalar.activation(
-                out=up_planes[:, half, h, :],
-                in_=up_ps[:].rearrange("p k l -> p (k l)"),
-                func=IDENTITY,
-                bias=bias_cols[:, h : h + 1],
+        up_grouped = const.tile([P, HALVES, TAPS, HALF_L, PACK], BF16, align_bytes=64)
+        up_codes = const.tile([P, HALVES, HALF_T], U32, align_bytes=64)
+        up_scales = const.tile([P, HALVES, HALF_T], U8, align_bytes=64)
+        bt_wide = bt_cols[:].unsqueeze(1).to_broadcast([P, HALF_L, PACK])
+
+        def add_bt(f, k):
+            nc.vector.tensor_tensor(
+                out=up_grouped[:, f, k],
+                in0=up_ps_tiles[k][:].rearrange("p h l -> p l h")[:, f * HALF_L : (f + 1) * HALF_L, :],
+                in1=bt_wide,
+                op=ADD,
             )
 
-        grouped_tiles = [regroup_wt(0)]
-        nc.scalar.copy(out=bias_cols[:], in_=bias_ps[:, :, 0])
-        up_ps_tiles = []
-        for u in range(UNITS):
-            if u + 1 < UNITS:
-                grouped_tiles.append(regroup_wt(u + 1))
-            up_ps_tiles.append(quantise_and_multiply(grouped_tiles[u]))
-            if u >= 1:
-                add_bt(u - 1, up_ps_tiles[u - 1])
-            if u + 1 == CHUNKS_BEFORE_W1 * HALVES:
-                transpose_w1()
-            if u == CHUNKS_BEFORE_W1 * HALVES:
-                regroup_w1()
-        quantise_w1()
-
-        up_grouped = const.tile([P, HALVES, HALF_T, PACK], BF16, align_bytes=64)
-        up_codes = const.tile([P, T], U32, align_bytes=64)
-        up_scales = const.tile([P, T], U8, align_bytes=64)
-        src = up_planes[:].rearrange("p f h (c i) -> p f c h i", i=4)
-        dst = up_grouped[:].rearrange("p f (c i) h -> p f c h i", i=4)
-        split = UP_VECTOR_STEPS // 4
-        nc.vector.tensor_copy(out=dst[:, 0], in_=src[:, 0])
-        add_bt(UNITS - 1, up_ps_tiles[UNITS - 1])
-        nc.vector.tensor_copy(out=dst[:, 1, 0:split], in_=src[:, 1, 0:split])
-        nc.scalar.copy(out=dst[:, 1, split : HALF_T // 4], in_=src[:, 1, split : HALF_T // 4])
-        for half in range(HALVES):
-            steps = slice(half * HALF_T, (half + 1) * HALF_T)
-            nc.vector.quantize_mx(
-                out=up_codes[:, steps].bitcast(FP8X4),
-                scales=up_scales[:, steps],
-                in_=up_grouped[:, half].rearrange("p s h -> p (s h)"),
-            )
-
-        out_rows = out.rearrange("j b n s -> (j b n) s")
-        for a in range(Y_TILES):
-            rows = slice(a * P, (a + 1) * P)
-            y_ps = psum_y.tile([P, T], F32)
-            for half in range(HALVES):
-                steps = slice(half * HALF_T, (half + 1) * HALF_T)
-                nc.tensor.matmul_mx(
-                    out=y_ps[:, steps],
-                    lhsT=w1_codes[:, rows].bitcast(FP8X4),
-                    lhsT_scale=w1_scales[:, rows],
-                    rhs=up_codes[:, steps].bitcast(FP8X4),
-                    rhs_scale=up_scales[:, steps],
-                    start=True,
-                    stop=True,
+        def add_bt_on_scalar(k):
+            up_planes = const.tile([P, PACK, L], BF16)
+            for h in range(PACK):
+                nc.scalar.activation(
+                    out=up_planes[:, h, :], in_=up_ps_tiles[k][:, h, :], func=IDENTITY, bias=bt_cols[:, h : h + 1]
                 )
-            y_sb = results.tile([P, T], F32)
+            nc.scalar.copy(
+                out=up_grouped[:, :, k], in_=up_planes[:].rearrange("p h (f l) -> p f l h", f=HALVES)
+            )
+
+        def quantise_up(f):
+            nc.vector.quantize_mx(
+                out=up_codes[:, f, :].bitcast(FP8X4),
+                scales=up_scales[:, f, :],
+                in_=up_grouped[:, f].rearrange("p k l h -> p (k l h)"),
+            )
+
+        out_rows = out.rearrange("j b n (r s) -> (j b n) r s", r=REPEAT)
+
+        def multiply_y(f, a):
+            rows = slice(a * P, (a + 1) * P)
+            y_ps = banks.tile([P, HALF_T], F32, tag="bank")
+            nc.tensor.matmul_mx(
+                out=y_ps[:],
+                lhsT=w1_codes[:, rows].bitcast(FP8X4),
+                lhsT_scale=w1_scales[:, rows],
+                rhs=up_codes[:, f, :].bitcast(FP8X4),
+                rhs_scale=up_scales[:, f, :],
+                start=True,
+                stop=True,
+            )
+            return y_ps
+
+        def store_y(f, a, y_ps, on_vector):
+            y_sb = results.tile([P, HALF_T], F32)
             y_in_time = y_sb[:].rearrange("p (l k) -> p l k", k=TAPS)
             y_by_tap = y_ps[:].rearrange("p (k l) -> p l k", k=TAPS)
-            b1_col = bias_cols[:, O_TILES + a : O_TILES + a + 1]
-            if a % 2 == 0:
-                nc.vector.tensor_scalar_add(out=y_in_time, in0=y_by_tap, scalar1=b1_col)
+            if on_vector:
+                nc.vector.tensor_scalar_add(out=y_in_time, in0=y_by_tap, scalar1=b1_cols[:, a : a + 1])
             else:
-                nc.scalar.activation(out=y_in_time, in_=y_by_tap, func=IDENTITY, bias=b1_col)
-            for r in range(REPEAT):
-                nc.sync.dma_start(out=out_rows[rows, r * T : (r + 1) * T], in_=y_sb[:])
+                nc.scalar.activation(out=y_in_time, in_=y_by_tap, func=IDENTITY, bias=b1_cols[:, a : a + 1])
+            nc.sync.dma_start(
+                out=out_rows[a * P : (a + 1) * P, :, f * HALF_T : (f + 1) * HALF_T],
+                in_=y_sb[:].unsqueeze(1).to_broadcast([P, REPEAT, HALF_T]),
+            )
+
+        add_bt_on_scalar(0)
+        for a in range(Y_TILES):
+            quantise_w1(a)
+        for k in range(1, TAPS):
+            add_bt(0, k)
+        quantise_up(0)
+        y_first = [multiply_y(0, a) for a in range(Y_TILES)]
+        store_y(0, 0, y_first[0], True)
+        store_y(0, 1, y_first[1], False)
+        store_y(0, 2, y_first[2], False)
+        for k in range(1, TAPS):
+            add_bt(1, k)
+        quantise_up(1)
+        for a in range(Y_TILES):
+            store_y(1, a, multiply_y(1, a), a % 2 == 0)

@@ -39,7 +39,7 @@ def tile_conditionalfeaturesupsample_s_kernel(tc, local_features, wt, bt, w1, b1
         ctx.enter_context(tc.manual_schedule())
         const = ctx.enter_context(tc.tile_pool(name="const", bufs=1))
         chunks = ctx.enter_context(tc.tile_pool(name="chunks", bufs=CHUNKS))
-        results = ctx.enter_context(tc.tile_pool(name="results", bufs=Y_TILES * HALVES))
+        results = ctx.enter_context(tc.tile_pool(name="results", bufs=Y_TILES))
         banks = ctx.enter_context(tc.psum_pool(name="banks", bufs=8))
 
         x_sb = const.tile([P, C], BF16)
@@ -210,31 +210,37 @@ def tile_conditionalfeaturesupsample_s_kernel(tc, local_features, wt, bt, w1, b1
             )
             return y_ps
 
-        def store_y(f, a, y_ps, on_vector):
-            y_sb = results.tile([P, HALF_T], F32)
-            y_in_time = y_sb[:].rearrange("p (l k) -> p l k", k=TAPS)
+        y_sb_tiles = [results.tile([P, T], F32, name="y_sb") for a in range(Y_TILES)]
+
+        def add_b1(f, a, y_ps, on_vector):
+            y_in_time = y_sb_tiles[a][:, f * HALF_T : (f + 1) * HALF_T].rearrange("p (l k) -> p l k", k=TAPS)
             y_by_tap = y_ps[:].rearrange("p (k l) -> p l k", k=TAPS)
             if on_vector:
                 nc.vector.tensor_scalar_add(out=y_in_time, in0=y_by_tap, scalar1=b1_cols[:, a : a + 1])
             else:
                 nc.scalar.activation(out=y_in_time, in_=y_by_tap, func=IDENTITY, bias=b1_cols[:, a : a + 1])
+
+        def store_y(a, first, last):
             nc.sync.dma_start(
-                out=out_rows[a * P : (a + 1) * P, :, f * HALF_T : (f + 1) * HALF_T],
-                in_=y_sb[:].unsqueeze(1).to_broadcast([P, REPEAT, HALF_T]),
+                out=out_rows[a * P : (a + 1) * P, :, first:last],
+                in_=y_sb_tiles[a][:, first:last].unsqueeze(1).to_broadcast([P, REPEAT, last - first]),
             )
 
         add_bt_on_scalar(0)
-        for a in range(Y_TILES):
-            quantise_w1(a)
+        quantise_w1(0)
+        quantise_w1(1)
         for k in range(1, TAPS):
             add_bt(0, k)
+        quantise_w1(2)
         quantise_up(0)
         y_first = [multiply_y(0, a) for a in range(Y_TILES)]
-        store_y(0, 0, y_first[0], True)
-        store_y(0, 1, y_first[1], False)
-        store_y(0, 2, y_first[2], False)
+        add_b1(0, 0, y_first[0], False)
+        store_y(0, 0, HALF_T)
+        add_b1(0, 1, y_first[1], False)
         for k in range(1, TAPS):
             add_bt(1, k)
+        add_b1(0, 2, y_first[2], True)
         quantise_up(1)
-        for a in range(Y_TILES):
-            store_y(1, a, multiply_y(1, a), a % 2 == 0)
+        for a, on_vector in ((1, True), (2, False), (0, True)):
+            add_b1(1, a, multiply_y(1, a), on_vector)
+            store_y(a, HALF_T if a == 0 else 0, T)

@@ -94,15 +94,16 @@ def tile_conditionalfeaturesupsample_s_kernel(tc, local_features, wt, bt, w1, b1
         wt_grouped = const.tile([P, TAPS, PACK, P, PACK], BF16, align_bytes=64)
         wt_by_channel = wt_grouped[:].rearrange("p k h m t -> p h m t k")
 
-        def regroup(copy, c, heads, taps):
-            cols = slice(c * CHUNK_M, (c + 1) * CHUNK_M)
+        def regroup(copy, c, heads, first, last):
+            cols = slice(c * CHUNK_M + first, c * CHUNK_M + last)
             src = wt_raw_tiles[c][:].rearrange("p t (m h k) -> p h m t k", h=PACK, k=TAPS)
-            copy(out=wt_by_channel[:, heads, cols, :, taps], in_=src[:, heads, :, :, taps])
+            copy(out=wt_by_channel[:, heads, cols], in_=src[:, heads, first:last])
 
         for c in range(CHUNKS):
-            regroup(nc.vector.tensor_copy, c, slice(0, PACK), slice(0, 2))
-            regroup(nc.scalar.copy, c, slice(1, PACK), slice(2, TAPS))
-            regroup(nc.vector.tensor_copy, c, slice(0, 1), slice(2, TAPS))
+            regroup(nc.vector.tensor_copy, c, slice(0, 2), 0, CHUNK_M)
+            regroup(nc.scalar.copy, c, slice(3, 4), 0, CHUNK_M)
+            regroup(nc.vector.tensor_copy, c, slice(2, 3), 0, CHUNK_M // 2)
+            regroup(nc.scalar.copy, c, slice(2, 3), CHUNK_M // 2, CHUNK_M)
 
         w1_words = w1_sb[:].rearrange("r a o -> r (a o)").bitcast(F32)
         w1_grouped = const.tile([P, OUT * PACK], BF16, align_bytes=64)

@@ -23,12 +23,13 @@ REPEAT = 4
 HEADS = 16
 LAYERS = OUT // HEADS
 Y_TILES = OUT // P
-CHUNKS = 4
-CHUNK_O = C // CHUNKS
-CHUNK_M = CHUNK_O // PACK
+CHUNK_SIZES = (192, 128, 128, 64)
+CHUNKS = len(CHUNK_SIZES)
 HALVES = 2
 HALF_L = L // HALVES
 HALF_T = T // HALVES
+
+WARM_COLS = 384
 
 FLOPS = 2 * L * C * C * TAPS + 2 * OUT * C * T
 
@@ -38,7 +39,6 @@ def tile_conditionalfeaturesupsample_s_kernel(tc, local_features, wt, bt, w1, b1
     with ExitStack() as ctx:
         ctx.enter_context(tc.manual_schedule())
         const = ctx.enter_context(tc.tile_pool(name="const", bufs=1))
-        chunks = ctx.enter_context(tc.tile_pool(name="chunks", bufs=CHUNKS))
         results = ctx.enter_context(tc.tile_pool(name="results", bufs=Y_TILES))
         banks = ctx.enter_context(tc.psum_pool(name="banks", bufs=8))
 
@@ -51,9 +51,10 @@ def tile_conditionalfeaturesupsample_s_kernel(tc, local_features, wt, bt, w1, b1
         wt_rows = wt.rearrange("(p t) o k -> p t (o k)", p=P)
         wt_raw_tiles = []
         for c in range(CHUNKS):
-            wt_raw = chunks.tile([P, PACK, CHUNK_O * TAPS], BF16)
+            first_o = sum(CHUNK_SIZES[:c])
+            wt_raw = const.tile([P, PACK, CHUNK_SIZES[c] * TAPS], BF16, name="wt_raw", tag="wt_raw_%d" % c)
             nc.sync.dma_start(
-                out=wt_raw[:], in_=wt_rows[:, :, c * CHUNK_O * TAPS : (c + 1) * CHUNK_O * TAPS]
+                out=wt_raw[:], in_=wt_rows[:, :, first_o * TAPS : (first_o + CHUNK_SIZES[c]) * TAPS]
             )
             wt_raw_tiles.append(wt_raw)
         w1_sb = const.tile([P, Y_TILES, C], BF16)
@@ -64,7 +65,7 @@ def tile_conditionalfeaturesupsample_s_kernel(tc, local_features, wt, bt, w1, b1
         nc.scalar.activation(out=warm[:, 1:2], in_=warm[:, 0:1], func=IDENTITY)
         ident = const.tile([P, P], F32)
         make_identity(nc, ident[:])
-        bias_rows = const.tile([P, OUT], F32)
+        bias_rows = const.tile([P, OUT], BF16)
         nc.gpsimd.memset(bias_rows[:], 0.0)
 
         x_words = x_sb[:].bitcast(F32)
@@ -84,26 +85,43 @@ def tile_conditionalfeaturesupsample_s_kernel(tc, local_features, wt, bt, w1, b1
             in_=b1_row[:].rearrange("a (n j) -> a j n", j=HEADS),
         )
         nc.vector.quantize_mx(out=x_codes[:].bitcast(FP8X4), scales=x_scales[:], in_=x_grouped[:])
+        warm_ps = banks.tile([P, WARM_COLS], F32, tag="bank")
+
+        def keep_busy(c):
+            words = wt_raw_tiles[c][:].rearrange("p t n -> p (t n)").bitcast(F32)
+            nc.tensor.matmul(warm_ps[:], lhsT=ident[:], rhs=words[:, 0:WARM_COLS], start=True, stop=True)
+
+        keep_busy(0)
+        unit = const.tile([P, 1], BF16)
+        nc.vector.tensor_copy(out=unit[:], in_=ident[:, 0:1])
         b1_ps = banks.tile([P, Y_TILES], F32, tag="bank")
         for a in range(Y_TILES):
             nc.tensor.matmul(
-                b1_ps[:, a : a + 1], lhsT=bias_rows[:, a * P : (a + 1) * P], rhs=ident[:, 0:1], start=True, stop=True
+                b1_ps[:, a : a + 1], lhsT=bias_rows[:, a * P : (a + 1) * P], rhs=unit[:], start=True, stop=True
             )
         b1_cols = const.tile([P, Y_TILES], F32)
+        for c in range(1, CHUNKS - 1):
+            keep_busy(c)
 
         wt_grouped = const.tile([P, TAPS, PACK, P, PACK], BF16, align_bytes=64)
         wt_by_channel = wt_grouped[:].rearrange("p k h m t -> p h m t k")
 
         def regroup(copy, c, heads, first, last):
-            cols = slice(c * CHUNK_M + first, c * CHUNK_M + last)
+            chunk_m = sum(CHUNK_SIZES[:c]) // PACK
+            cols = slice(chunk_m + first, chunk_m + last)
             src = wt_raw_tiles[c][:].rearrange("p t (m h k) -> p h m t k", h=PACK, k=TAPS)
             copy(out=wt_by_channel[:, heads, cols], in_=src[:, heads, first:last])
 
         for c in range(CHUNKS):
-            regroup(nc.vector.tensor_copy, c, slice(0, 2), 0, CHUNK_M)
-            regroup(nc.scalar.copy, c, slice(3, 4), 0, CHUNK_M)
-            regroup(nc.vector.tensor_copy, c, slice(2, 3), 0, CHUNK_M // 2)
-            regroup(nc.scalar.copy, c, slice(2, 3), CHUNK_M // 2, CHUNK_M)
+            size = CHUNK_SIZES[c] // PACK
+            regroup(nc.vector.tensor_copy, c, slice(0, 2), 0, size)
+            if c < CHUNKS - 1:
+                regroup(nc.scalar.copy, c, slice(3, 4), 0, size)
+                regroup(nc.vector.tensor_copy, c, slice(2, 3), 0, size // 2)
+                regroup(nc.scalar.copy, c, slice(2, 3), size // 2, size)
+            else:
+                nc.scalar.copy(out=b1_cols[:], in_=b1_ps[:])
+                regroup(nc.scalar.copy, c, slice(2, 4), 0, size)
 
         w1_words = w1_sb[:].rearrange("r a o -> r (a o)").bitcast(F32)
         w1_grouped = const.tile([P, OUT * PACK], BF16, align_bytes=64)
@@ -121,7 +139,6 @@ def tile_conditionalfeaturesupsample_s_kernel(tc, local_features, wt, bt, w1, b1
                 out=w1_by_head[:, :, a * layers_per_tile : (a + 1) * layers_per_tile, :],
                 in_=w1_ps_tiles[a][:].rearrange("p u (n j) -> p j n u", j=HEADS),
             )
-        nc.scalar.copy(out=b1_cols[:], in_=b1_ps[:])
         w1_codes = const.tile([P, OUT], U32, align_bytes=64)
         w1_scales = const.tile([P, OUT], U8, align_bytes=64)
 
@@ -135,7 +152,6 @@ def tile_conditionalfeaturesupsample_s_kernel(tc, local_features, wt, bt, w1, b1
 
         wt_codes = const.tile([P, TAPS, C], U32, align_bytes=64)
         wt_scales = const.tile([P, TAPS, C], U8, align_bytes=64)
-        up_ps_tiles = []
 
         def quantise_and_multiply(k, up_ps, heads):
             cols = slice(heads[0] * P, (heads[-1] + 1) * P)
@@ -156,14 +172,11 @@ def tile_conditionalfeaturesupsample_s_kernel(tc, local_features, wt, bt, w1, b1
                     stop=True,
                 )
 
-        for k in range(TAPS):
-            up_ps = banks.tile([P, PACK, L], F32, tag="bank")
-            if k < TAPS - 1:
-                quantise_and_multiply(k, up_ps, range(PACK))
-            else:
-                quantise_and_multiply(k, up_ps, range(PACK // 2))
-                quantise_and_multiply(k, up_ps, range(PACK // 2, PACK))
-            up_ps_tiles.append(up_ps)
+        up_ps_tiles = [banks.tile([P, PACK, L], F32, tag="bank", name="up_ps") for k in range(TAPS)]
+        for pair in (range(0, 2), range(2, TAPS)):
+            for heads in (range(PACK // 2), range(PACK // 2, PACK)):
+                for k in pair:
+                    quantise_and_multiply(k, up_ps_tiles[k], heads)
 
         up_grouped = const.tile([P, HALVES, TAPS, HALF_L, PACK], BF16, align_bytes=64)
         up_codes = const.tile([P, HALVES, HALF_T], U32, align_bytes=64)
@@ -235,13 +248,13 @@ def tile_conditionalfeaturesupsample_s_kernel(tc, local_features, wt, bt, w1, b1
         quantise_w1(2)
         quantise_up(0)
         y_first = [multiply_y(0, a) for a in range(Y_TILES)]
-        add_b1(0, 0, y_first[0], False)
-        store_y(0, 0, HALF_T)
-        add_b1(0, 1, y_first[1], False)
+        for a in range(2):
+            add_b1(0, a, y_first[a], False)
+            store_y(a, 0, HALF_T)
         for k in range(1, TAPS):
             add_bt(1, k)
         add_b1(0, 2, y_first[2], True)
         quantise_up(1)
-        for a, on_vector in ((1, True), (2, False), (0, True)):
+        for a, on_vector in ((2, True), (0, False), (1, True)):
             add_b1(1, a, multiply_y(1, a), on_vector)
-            store_y(a, HALF_T if a == 0 else 0, T)
+            store_y(a, 0 if a == 2 else HALF_T, T)

@@ -25,9 +25,7 @@ LAYERS = OUT // HEADS
 Y_TILES = OUT // P
 CHUNK_SIZES = (192, 128, 128, 64)
 CHUNKS = len(CHUNK_SIZES)
-HALVES = 2
-HALF_L = L // HALVES
-HALF_T = T // HALVES
+PARTS = ((0, 32), (32, 96), (96, 128))
 
 WARM_COLS = 384
 
@@ -39,6 +37,7 @@ def tile_conditionalfeaturesupsample_s_kernel(tc, local_features, wt, bt, w1, b1
     with ExitStack() as ctx:
         ctx.enter_context(tc.manual_schedule())
         const = ctx.enter_context(tc.tile_pool(name="const", bufs=1))
+        planes = ctx.enter_context(tc.tile_pool(name="planes", bufs=2))
         results = ctx.enter_context(tc.tile_pool(name="results", bufs=Y_TILES))
         banks = ctx.enter_context(tc.psum_pool(name="banks", bufs=8))
 
@@ -46,8 +45,6 @@ def tile_conditionalfeaturesupsample_s_kernel(tc, local_features, wt, bt, w1, b1
         nc.sync.dma_start(out=x_sb[:], in_=local_features[0])
         b1_row = const.tile([1, OUT], BF16)
         nc.scalar.dma_start(out=b1_row[:], in_=b1.rearrange("(a c) -> a c", a=1))
-        bt_cols = const.tile([P, PACK], BF16)
-        nc.scalar.dma_start(out=bt_cols[:], in_=bt.rearrange("(p t) -> p t", t=PACK))
         wt_rows = wt.rearrange("(p t) o k -> p t (o k)", p=P)
         wt_raw_tiles = []
         for c in range(CHUNKS):
@@ -59,6 +56,8 @@ def tile_conditionalfeaturesupsample_s_kernel(tc, local_features, wt, bt, w1, b1
             wt_raw_tiles.append(wt_raw)
         w1_sb = const.tile([P, Y_TILES, C], BF16)
         nc.sync.dma_start(out=w1_sb[:], in_=w1.rearrange("(a r) o -> r a o", r=P))
+        bt_cols = const.tile([P, PACK], BF16)
+        nc.sync.dma_start(out=bt_cols[:], in_=bt.rearrange("(p t) -> p t", t=PACK))
 
         warm = const.tile([P, 2], F32)
         nc.vector.memset(warm[:, 0:1], 0.0)
@@ -178,47 +177,59 @@ def tile_conditionalfeaturesupsample_s_kernel(tc, local_features, wt, bt, w1, b1
                 for k in pair:
                     quantise_and_multiply(k, up_ps_tiles[k], heads)
 
-        up_grouped = const.tile([P, HALVES, TAPS, HALF_L, PACK], BF16, align_bytes=64)
-        up_codes = const.tile([P, HALVES, HALF_T], U32, align_bytes=64)
-        up_scales = const.tile([P, HALVES, HALF_T], U8, align_bytes=64)
-        bt_wide = bt_cols[:].unsqueeze(1).to_broadcast([P, HALF_L, PACK])
+        up_grouped = const.tile([P, T * PACK], BF16, align_bytes=64)
+        up_codes = const.tile([P, T], U32, align_bytes=64)
+        up_scales = const.tile([P, T], U8, align_bytes=64)
+
+        def grouped_part(f):
+            first, last = PARTS[f]
+            part = up_grouped[:, first * TAPS * PACK : last * TAPS * PACK]
+            return part.rearrange("p (k l h) -> p k l h", k=TAPS, h=PACK)
 
         def add_bt(f, k):
+            first, last = PARTS[f]
             nc.vector.tensor_tensor(
-                out=up_grouped[:, f, k],
-                in0=up_ps_tiles[k][:].rearrange("p h l -> p l h")[:, f * HALF_L : (f + 1) * HALF_L, :],
-                in1=bt_wide,
+                out=grouped_part(f)[:, k],
+                in0=up_ps_tiles[k][:].rearrange("p h l -> p l h")[:, first:last, :],
+                in1=bt_cols[:].unsqueeze(1).to_broadcast([P, last - first, PACK]),
                 op=ADD,
             )
 
-        def add_bt_on_scalar(k):
-            up_planes = const.tile([P, PACK, L], BF16)
+        def add_bt_on_scalar(k, parts):
+            up_planes = planes.tile([P, PACK, L], BF16)
+            first = PARTS[parts[0]][0]
             for h in range(PACK):
                 nc.scalar.activation(
-                    out=up_planes[:, h, :], in_=up_ps_tiles[k][:, h, :], func=IDENTITY, bias=bt_cols[:, h : h + 1]
+                    out=up_planes[:, h, first:], in_=up_ps_tiles[k][:, h, first:], func=IDENTITY, bias=bt_cols[:, h : h + 1]
                 )
-            nc.scalar.copy(
-                out=up_grouped[:, :, k], in_=up_planes[:].rearrange("p h (f l) -> p f l h", f=HALVES)
-            )
+            for f in parts:
+                first, last = PARTS[f]
+                nc.scalar.copy(
+                    out=grouped_part(f)[:, k], in_=up_planes[:, :, first:last].rearrange("p h l -> p l h")
+                )
 
         def quantise_up(f):
+            first, last = PARTS[f]
+            cols = slice(first * TAPS, last * TAPS)
             nc.vector.quantize_mx(
-                out=up_codes[:, f, :].bitcast(FP8X4),
-                scales=up_scales[:, f, :],
-                in_=up_grouped[:, f].rearrange("p k l h -> p (k l h)"),
+                out=up_codes[:, cols].bitcast(FP8X4),
+                scales=up_scales[:, cols],
+                in_=up_grouped[:, first * TAPS * PACK : last * TAPS * PACK],
             )
 
         out_rows = out.rearrange("j b n (r s) -> (j b n) r s", r=REPEAT)
 
         def multiply_y(f, a):
             rows = slice(a * P, (a + 1) * P)
-            y_ps = banks.tile([P, HALF_T], F32, tag="bank")
+            first, last = PARTS[f]
+            cols = slice(first * TAPS, last * TAPS)
+            y_ps = banks.tile([P, (last - first) * TAPS], F32, tag="bank")
             nc.tensor.matmul_mx(
                 out=y_ps[:],
                 lhsT=w1_codes[:, rows].bitcast(FP8X4),
                 lhsT_scale=w1_scales[:, rows],
-                rhs=up_codes[:, f, :].bitcast(FP8X4),
-                rhs_scale=up_scales[:, f, :],
+                rhs=up_codes[:, cols].bitcast(FP8X4),
+                rhs_scale=up_scales[:, cols],
                 start=True,
                 stop=True,
             )
@@ -227,34 +238,50 @@ def tile_conditionalfeaturesupsample_s_kernel(tc, local_features, wt, bt, w1, b1
         y_sb_tiles = [results.tile([P, T], F32, name="y_sb") for a in range(Y_TILES)]
 
         def add_b1(f, a, y_ps, on_vector):
-            y_in_time = y_sb_tiles[a][:, f * HALF_T : (f + 1) * HALF_T].rearrange("p (l k) -> p l k", k=TAPS)
+            first, last = PARTS[f]
+            y_in_time = y_sb_tiles[a][:, first * TAPS : last * TAPS].rearrange("p (l k) -> p l k", k=TAPS)
             y_by_tap = y_ps[:].rearrange("p (k l) -> p l k", k=TAPS)
             if on_vector:
                 nc.vector.tensor_scalar_add(out=y_in_time, in0=y_by_tap, scalar1=b1_cols[:, a : a + 1])
             else:
                 nc.scalar.activation(out=y_in_time, in_=y_by_tap, func=IDENTITY, bias=b1_cols[:, a : a + 1])
 
-        def store_y(a, first, last):
+        def store_y(a, first_part, last_part):
+            steps = slice(PARTS[first_part][0] * TAPS, PARTS[last_part][1] * TAPS)
             nc.sync.dma_start(
-                out=out_rows[a * P : (a + 1) * P, :, first:last],
-                in_=y_sb_tiles[a][:, first:last].unsqueeze(1).to_broadcast([P, REPEAT, last - first]),
+                out=out_rows[a * P : (a + 1) * P, :, steps],
+                in_=y_sb_tiles[a][:, steps].unsqueeze(1).to_broadcast([P, REPEAT, steps.stop - steps.start]),
             )
 
-        add_bt_on_scalar(0)
+        add_bt_on_scalar(0, (0, 1, 2))
         quantise_w1(0)
         quantise_w1(1)
         for k in range(1, TAPS):
             add_bt(0, k)
-        quantise_w1(2)
+            if k == 1:
+                add_bt_on_scalar(1, (1, 2))
         quantise_up(0)
-        y_first = [multiply_y(0, a) for a in range(Y_TILES)]
-        for a in range(2):
-            add_b1(0, a, y_first[a], False)
-            store_y(a, 0, HALF_T)
-        for k in range(1, TAPS):
+        y_first = [multiply_y(0, a) for a in range(2)]
+        quantise_w1(2)
+        y_first.append(multiply_y(0, 2))
+        for k in range(2, TAPS):
             add_bt(1, k)
-        add_b1(0, 2, y_first[2], True)
+        for a in range(Y_TILES):
+            add_b1(0, a, y_first[a], False)
+            store_y(a, 0, 0)
         quantise_up(1)
-        for a, on_vector in ((2, True), (0, False), (1, True)):
-            add_b1(1, a, multiply_y(1, a), on_vector)
-            store_y(a, 0 if a == 2 else HALF_T, T)
+        y_second = [multiply_y(1, a) for a in range(Y_TILES)]
+        for k in range(2, TAPS):
+            add_bt(2, k)
+        add_b1(1, 0, y_second[0], False)
+        store_y(0, 1, 1)
+        add_b1(1, 1, y_second[1], False)
+        quantise_up(2)
+        y_third = [multiply_y(2, a) for a in range(Y_TILES)]
+        add_b1(1, 2, y_second[2], True)
+        add_b1(2, 1, y_third[1], False)
+        store_y(1, 1, 2)
+        add_b1(2, 2, y_third[2], True)
+        store_y(2, 1, 2)
+        add_b1(2, 0, y_third[0], False)
+        store_y(0, 2, 2)

@@ -25,7 +25,8 @@ LAYERS = OUT // HEADS
 Y_TILES = OUT // P
 CHUNK_SIZES = (192, 128, 128, 64)
 CHUNKS = len(CHUNK_SIZES)
-PARTS = ((0, 32), (32, 96), (96, 128))
+PARTS = ((0, 64), (64, 128))
+WIDE_TILE = 2
 
 WARM_COLS = 384
 
@@ -38,7 +39,7 @@ def tile_conditionalfeaturesupsample_s_kernel(tc, local_features, wt, bt, w1, b1
         ctx.enter_context(tc.manual_schedule())
         const = ctx.enter_context(tc.tile_pool(name="const", bufs=1))
         planes = ctx.enter_context(tc.tile_pool(name="planes", bufs=2))
-        results = ctx.enter_context(tc.tile_pool(name="results", bufs=Y_TILES))
+        results = ctx.enter_context(tc.tile_pool(name="results", bufs=1))
         banks = ctx.enter_context(tc.psum_pool(name="banks", bufs=8))
 
         x_sb = const.tile([P, C], BF16)
@@ -235,11 +236,14 @@ def tile_conditionalfeaturesupsample_s_kernel(tc, local_features, wt, bt, w1, b1
             )
             return y_ps
 
-        y_sb_tiles = [results.tile([P, T], F32, name="y_sb") for a in range(Y_TILES)]
+        y_sb_tiles = [
+            results.tile([P, REPEAT if a == WIDE_TILE else 1, T], F32, name="y_sb", tag="y_sb_%d" % a)
+            for a in range(Y_TILES)
+        ]
 
         def add_b1(f, a, y_ps, on_vector):
             first, last = PARTS[f]
-            y_in_time = y_sb_tiles[a][:, first * TAPS : last * TAPS].rearrange("p (l k) -> p l k", k=TAPS)
+            y_in_time = y_sb_tiles[a][:, 0, first * TAPS : last * TAPS].rearrange("p (l k) -> p l k", k=TAPS)
             y_by_tap = y_ps[:].rearrange("p (k l) -> p l k", k=TAPS)
             if on_vector:
                 nc.vector.tensor_scalar_add(out=y_in_time, in0=y_by_tap, scalar1=b1_cols[:, a : a + 1])
@@ -250,38 +254,37 @@ def tile_conditionalfeaturesupsample_s_kernel(tc, local_features, wt, bt, w1, b1
             steps = slice(PARTS[first_part][0] * TAPS, PARTS[last_part][1] * TAPS)
             nc.sync.dma_start(
                 out=out_rows[a * P : (a + 1) * P, :, steps],
-                in_=y_sb_tiles[a][:, steps].unsqueeze(1).to_broadcast([P, REPEAT, steps.stop - steps.start]),
+                in_=y_sb_tiles[a][:, :, steps].to_broadcast([P, REPEAT, steps.stop - steps.start]),
             )
 
-        add_bt_on_scalar(0, (0, 1, 2))
+        add_bt_on_scalar(0, (0, 1))
         quantise_w1(0)
         quantise_w1(1)
         for k in range(1, TAPS):
             add_bt(0, k)
             if k == 1:
-                add_bt_on_scalar(1, (1, 2))
-        quantise_up(0)
-        y_first = [multiply_y(0, a) for a in range(2)]
+                add_bt_on_scalar(1, (1,))
         quantise_w1(2)
-        y_first.append(multiply_y(0, 2))
+        quantise_up(0)
+        y_first = [multiply_y(0, a) for a in range(Y_TILES)]
+        add_b1(0, 0, y_first[0], False)
+        store_y(0, 0, 0)
         for k in range(2, TAPS):
             add_bt(1, k)
-        for a in range(Y_TILES):
-            add_b1(0, a, y_first[a], False)
-            store_y(a, 0, 0)
+        add_b1(0, 1, y_first[1], False)
+        add_b1(0, 2, y_first[2], False)
         quantise_up(1)
-        y_second = [multiply_y(1, a) for a in range(Y_TILES)]
-        for k in range(2, TAPS):
-            add_bt(2, k)
+        y_second = {a: multiply_y(1, a) for a in (1, 2, 0)}
+        add_b1(1, 1, y_second[1], True)
+        store_y(1, 0, 1)
+        add_b1(1, 2, y_second[2], False)
+        y_wide = y_sb_tiles[WIDE_TILE]
+        nc.vector.tensor_copy(out=y_wide[:, 1, :], in_=y_wide[:, 0, :])
+        nc.scalar.copy(out=y_wide[:, 2, :], in_=y_wide[:, 0, :])
+        nc.vector.tensor_copy(out=y_wide[:, 3, :], in_=y_wide[:, 0, :])
+        nc.sync.dma_start(
+            out=out_rows[WIDE_TILE * P : (WIDE_TILE + 1) * P].rearrange("q r s -> q (r s)"),
+            in_=y_wide[:].rearrange("p r s -> p (r s)"),
+        )
         add_b1(1, 0, y_second[0], False)
         store_y(0, 1, 1)
-        add_b1(1, 1, y_second[1], False)
-        quantise_up(2)
-        y_third = [multiply_y(2, a) for a in range(Y_TILES)]
-        add_b1(1, 2, y_second[2], True)
-        add_b1(2, 1, y_third[1], False)
-        store_y(1, 1, 2)
-        add_b1(2, 2, y_third[2], True)
-        store_y(2, 1, 2)
-        add_b1(2, 0, y_third[0], False)
-        store_y(0, 2, 2)

@@ -28,7 +28,8 @@ CHUNKS = len(CHUNK_SIZES)
 PARTS = ((0, 64), (64, 128))
 WIDE_TILE = 2
 
-WARM_COLS = 384
+LOAD_COLS = 256
+UP_COLS = 384
 
 FLOPS = 2 * L * C * C * TAPS + 2 * OUT * C * T
 
@@ -85,13 +86,12 @@ def tile_conditionalfeaturesupsample_s_kernel(tc, local_features, wt, bt, w1, b1
             in_=b1_row[:].rearrange("a (n j) -> a j n", j=HEADS),
         )
         nc.vector.quantize_mx(out=x_codes[:].bitcast(FP8X4), scales=x_scales[:], in_=x_grouped[:])
-        warm_ps = banks.tile([P, WARM_COLS], F32, tag="bank")
-
-        def keep_busy(c):
+        def keep_busy(c, columns):
+            idle_ps = banks.tile([P, columns], F32, tag="bank")
             words = wt_raw_tiles[c][:].rearrange("p t n -> p (t n)").bitcast(F32)
-            nc.tensor.matmul(warm_ps[:], lhsT=ident[:], rhs=words[:, 0:WARM_COLS], start=True, stop=True)
+            nc.tensor.matmul(idle_ps[:], lhsT=ident[:], rhs=words[:, 0:columns], start=True, stop=True)
 
-        keep_busy(0)
+        keep_busy(0, LOAD_COLS)
         unit = const.tile([P, 1], BF16)
         nc.vector.tensor_copy(out=unit[:], in_=ident[:, 0:1])
         b1_ps = banks.tile([P, Y_TILES], F32, tag="bank")
@@ -100,8 +100,8 @@ def tile_conditionalfeaturesupsample_s_kernel(tc, local_features, wt, bt, w1, b1
                 b1_ps[:, a : a + 1], lhsT=bias_rows[:, a * P : (a + 1) * P], rhs=unit[:], start=True, stop=True
             )
         b1_cols = const.tile([P, Y_TILES], F32)
-        for c in range(1, CHUNKS - 1):
-            keep_busy(c)
+        for c in range(1, CHUNKS):
+            keep_busy(c, LOAD_COLS)
 
         wt_grouped = const.tile([P, TAPS, PACK, P, PACK], BF16, align_bytes=64)
         wt_by_channel = wt_grouped[:].rearrange("p k h m t -> p h m t k")
@@ -177,6 +177,8 @@ def tile_conditionalfeaturesupsample_s_kernel(tc, local_features, wt, bt, w1, b1
             for heads in (range(PACK // 2), range(PACK // 2, PACK)):
                 for k in pair:
                     quantise_and_multiply(k, up_ps_tiles[k], heads)
+
+        keep_busy(0, UP_COLS)
 
         up_grouped = const.tile([P, T * PACK], BF16, align_bytes=64)
         up_codes = const.tile([P, T], U32, align_bytes=64)

@@ -26,7 +26,7 @@ Y_TILES = OUT // P
 CHUNK_SIZES = (192, 128, 128, 64)
 CHUNKS = len(CHUNK_SIZES)
 PARTS = ((0, 64), (64, 128))
-WIDE_TILE = 2
+SPLIT_TILE = 0
 
 LOAD_COLS = 256
 UP_COLS = 384
@@ -239,7 +239,7 @@ def tile_conditionalfeaturesupsample_s_kernel(tc, local_features, wt, bt, w1, b1
             return y_ps
 
         y_sb_tiles = [
-            results.tile([P, REPEAT if a == WIDE_TILE else 1, T], F32, name="y_sb", tag="y_sb_%d" % a)
+            results.tile([P, 1 if a == SPLIT_TILE else REPEAT, T], F32, name="y_sb", tag="y_sb_%d" % a)
             for a in range(Y_TILES)
         ]
 
@@ -252,41 +252,45 @@ def tile_conditionalfeaturesupsample_s_kernel(tc, local_features, wt, bt, w1, b1
             else:
                 nc.scalar.activation(out=y_in_time, in_=y_by_tap, func=IDENTITY, bias=b1_cols[:, a : a + 1])
 
-        def store_y(a, first_part, last_part):
-            steps = slice(PARTS[first_part][0] * TAPS, PARTS[last_part][1] * TAPS)
+        def store_part(f):
+            steps = slice(PARTS[f][0] * TAPS, PARTS[f][1] * TAPS)
             nc.sync.dma_start(
-                out=out_rows[a * P : (a + 1) * P, :, steps],
-                in_=y_sb_tiles[a][:, :, steps].to_broadcast([P, REPEAT, steps.stop - steps.start]),
+                out=out_rows[SPLIT_TILE * P : (SPLIT_TILE + 1) * P, :, steps],
+                in_=y_sb_tiles[SPLIT_TILE][:, :, steps].to_broadcast([P, REPEAT, steps.stop - steps.start]),
+            )
+
+        def store_whole(a):
+            nc.sync.dma_start(
+                out=out_rows[a * P : (a + 1) * P].rearrange("q r s -> q (r s)"),
+                in_=y_sb_tiles[a][:].rearrange("p r s -> p (r s)"),
             )
 
         add_bt_on_scalar(0, (0, 1))
-        quantise_w1(0)
-        quantise_w1(1)
         for k in range(1, TAPS):
             add_bt(0, k)
             if k == 1:
                 add_bt_on_scalar(1, (1,))
-        quantise_w1(2)
+        quantise_w1(0)
         quantise_up(0)
-        y_first = [multiply_y(0, a) for a in range(Y_TILES)]
+        y_first = [multiply_y(0, 0)]
         add_b1(0, 0, y_first[0], False)
-        store_y(0, 0, 0)
+        store_part(0)
         for k in range(2, TAPS):
             add_bt(1, k)
-        add_b1(0, 1, y_first[1], False)
-        add_b1(0, 2, y_first[2], False)
+            a = k - 1
+            quantise_w1(a)
+            y_first.append(multiply_y(0, a))
+            add_b1(0, a, y_first[a], False)
         quantise_up(1)
-        y_second = {a: multiply_y(1, a) for a in (1, 2, 0)}
-        add_b1(1, 1, y_second[1], True)
-        store_y(1, 0, 1)
-        add_b1(1, 2, y_second[2], False)
-        y_wide = y_sb_tiles[WIDE_TILE]
-        nc.vector.tensor_copy(out=y_wide[:, 1, :], in_=y_wide[:, 0, :])
-        nc.scalar.copy(out=y_wide[:, 2, :], in_=y_wide[:, 0, :])
-        nc.vector.tensor_copy(out=y_wide[:, 3, :], in_=y_wide[:, 0, :])
-        nc.sync.dma_start(
-            out=out_rows[WIDE_TILE * P : (WIDE_TILE + 1) * P].rearrange("q r s -> q (r s)"),
-            in_=y_wide[:].rearrange("p r s -> p (r s)"),
-        )
-        add_b1(1, 0, y_second[0], False)
-        store_y(0, 1, 1)
+        y_second = [multiply_y(1, a) for a in range(Y_TILES)]
+        add_b1(1, 0, y_second[0], True)
+        store_part(1)
+        add_b1(1, 1, y_second[1], False)
+        for a in range(1, Y_TILES):
+            y_sb = y_sb_tiles[a]
+            nc.vector.tensor_copy(out=y_sb[:, 1, :], in_=y_sb[:, 0, :])
+            nc.scalar.copy(out=y_sb[:, 2, :], in_=y_sb[:, 0, :])
+            nc.vector.tensor_copy(out=y_sb[:, 3, :], in_=y_sb[:, 0, :])
+            store_whole(a)
+            if a == 1:
+                add_b1(1, 2, y_second[2], True)

from contextlib import ExitStack

import concourse.mybir as mybir
from concourse.masks import make_identity

BF16 = mybir.dt.bfloat16
F32 = mybir.dt.float32
U32 = mybir.dt.uint32
U8 = mybir.dt.uint8
FP8X4 = mybir.dt.float8_e4m3fn_x4
IDENTITY = mybir.ActivationFunctionType.Identity
ADD = mybir.AluOpType.add

P = 128
PACK = 4
PAIRS = 2
L = 128
C = 512
TAPS = 4
T = L * TAPS
OUT = 384
REPEAT = 4
HEADS = 16
LAYERS = OUT // HEADS
Y_TILES = OUT // P
CHUNK_SIZES = (192, 128, 128, 64)
CHUNKS = len(CHUNK_SIZES)
PARTS = ((0, 64), (64, 128))
SPLIT_TILE = 0

LOAD_COLS = 256
UP_COLS = 384

FLOPS = 2 * L * C * C * TAPS + 2 * OUT * C * T


def tile_conditionalfeaturesupsample_s_kernel(tc, local_features, wt, bt, w1, b1, out):
    nc = tc.nc
    with ExitStack() as ctx:
        ctx.enter_context(tc.manual_schedule())
        const = ctx.enter_context(tc.tile_pool(name="const", bufs=1))
        planes = ctx.enter_context(tc.tile_pool(name="planes", bufs=2))
        results = ctx.enter_context(tc.tile_pool(name="results", bufs=1))
        banks = ctx.enter_context(tc.psum_pool(name="banks", bufs=8))

        x_sb = const.tile([P, C], BF16)
        nc.sync.dma_start(out=x_sb[:], in_=local_features[0])
        b1_row = const.tile([1, OUT], BF16)
        nc.scalar.dma_start(out=b1_row[:], in_=b1.rearrange("(a c) -> a c", a=1))
        wt_rows = wt.rearrange("(p t) o k -> p t (o k)", p=P)
        wt_raw_tiles = []
        for c in range(CHUNKS):
            first_o = sum(CHUNK_SIZES[:c])
            wt_raw = const.tile([P, PACK, CHUNK_SIZES[c] * TAPS], BF16, name="wt_raw", tag="wt_raw_%d" % c)
            nc.sync.dma_start(
                out=wt_raw[:], in_=wt_rows[:, :, first_o * TAPS : (first_o + CHUNK_SIZES[c]) * TAPS]
            )
            wt_raw_tiles.append(wt_raw)
        w1_sb = const.tile([P, Y_TILES, C], BF16)
        nc.sync.dma_start(out=w1_sb[:], in_=w1.rearrange("(a r) o -> r a o", r=P))
        bt_cols = const.tile([P, PACK], BF16)
        nc.sync.dma_start(out=bt_cols[:], in_=bt.rearrange("(p t) -> p t", t=PACK))

        warm = const.tile([P, 2], F32)
        nc.vector.memset(warm[:, 0:1], 0.0)
        nc.scalar.activation(out=warm[:, 1:2], in_=warm[:, 0:1], func=IDENTITY)
        ident = const.tile([P, P], F32)
        make_identity(nc, ident[:])
        bias_rows = const.tile([P, OUT], BF16)
        nc.gpsimd.memset(bias_rows[:], 0.0)

        x_words = x_sb[:].bitcast(F32)
        x_ps = banks.tile([P, PAIRS, L], F32, tag="bank")
        for u in range(PAIRS):
            nc.tensor.transpose(x_ps[:, u, :], x_words[:, u : C // 2 : PAIRS], ident[:])
        x_grouped = const.tile([P, L * PACK], BF16, align_bytes=64)
        nc.scalar.copy(
            out=x_grouped[:].bitcast(F32).rearrange("p (l u) -> p l u", u=PAIRS),
            in_=x_ps[:].rearrange("p u l -> p l u"),
        )
        x_codes = const.tile([P, L], U32, align_bytes=64)
        x_scales = const.tile([P, L], U8, align_bytes=64)

        nc.vector.tensor_copy(
            out=bias_rows[0:1, :].rearrange("a (j n) -> a j n", j=HEADS),
            in_=b1_row[:].rearrange("a (n j) -> a j n", j=HEADS),
        )
        nc.vector.quantize_mx(out=x_codes[:].bitcast(FP8X4), scales=x_scales[:], in_=x_grouped[:])
        def keep_busy(c, columns):
            idle_ps = banks.tile([P, columns], F32, tag="bank")
            words = wt_raw_tiles[c][:].rearrange("p t n -> p (t n)").bitcast(F32)
            nc.tensor.matmul(idle_ps[:], lhsT=ident[:], rhs=words[:, 0:columns], start=True, stop=True)

        keep_busy(0, LOAD_COLS)
        unit = const.tile([P, 1], BF16)
        nc.vector.tensor_copy(out=unit[:], in_=ident[:, 0:1])
        b1_ps = banks.tile([P, Y_TILES], F32, tag="bank")
        for a in range(Y_TILES):
            nc.tensor.matmul(
                b1_ps[:, a : a + 1], lhsT=bias_rows[:, a * P : (a + 1) * P], rhs=unit[:], start=True, stop=True
            )
        b1_cols = const.tile([P, Y_TILES], F32)
        for c in range(1, CHUNKS):
            keep_busy(c, LOAD_COLS)

        wt_grouped = const.tile([P, TAPS, PACK, P, PACK], BF16, align_bytes=64)
        wt_by_channel = wt_grouped[:].rearrange("p k h m t -> p h m t k")

        def regroup(copy, c, heads, first, last):
            chunk_m = sum(CHUNK_SIZES[:c]) // PACK
            cols = slice(chunk_m + first, chunk_m + last)
            src = wt_raw_tiles[c][:].rearrange("p t (m h k) -> p h m t k", h=PACK, k=TAPS)
            copy(out=wt_by_channel[:, heads, cols], in_=src[:, heads, first:last])

        for c in range(CHUNKS):
            size = CHUNK_SIZES[c] // PACK
            regroup(nc.vector.tensor_copy, c, slice(0, 2), 0, size)
            if c < CHUNKS - 1:
                regroup(nc.scalar.copy, c, slice(3, 4), 0, size)
                regroup(nc.vector.tensor_copy, c, slice(2, 3), 0, size // 2)
                regroup(nc.scalar.copy, c, slice(2, 3), size // 2, size)
            else:
                nc.scalar.copy(out=b1_cols[:], in_=b1_ps[:])
                regroup(nc.scalar.copy, c, slice(2, 4), 0, size)

        w1_words = w1_sb[:].rearrange("r a o -> r (a o)").bitcast(F32)
        w1_grouped = const.tile([P, OUT * PACK], BF16, align_bytes=64)
        w1_by_head = w1_grouped[:].bitcast(F32).rearrange("p (j n u) -> p j n u", j=HEADS, u=PAIRS)
        layers_per_tile = P // HEADS
        w1_ps_tiles = []
        for a in range(Y_TILES):
            w1_ps = banks.tile([P, PAIRS, P], F32, tag="bank")
            first = a * (C // 2)
            for u in range(PAIRS):
                nc.tensor.transpose(w1_ps[:, u, :], w1_words[:, first + u : first + C // 2 : PAIRS], ident[:])
            w1_ps_tiles.append(w1_ps)
        for a in range(Y_TILES):
            nc.scalar.copy(
                out=w1_by_head[:, :, a * layers_per_tile : (a + 1) * layers_per_tile, :],
                in_=w1_ps_tiles[a][:].rearrange("p u (n j) -> p j n u", j=HEADS),
            )
        w1_codes = const.tile([P, OUT], U32, align_bytes=64)
        w1_scales = const.tile([P, OUT], U8, align_bytes=64)

        def quantise_w1(a):
            rows = slice(a * P, (a + 1) * P)
            nc.vector.quantize_mx(
                out=w1_codes[:, rows].bitcast(FP8X4),
                scales=w1_scales[:, rows],
                in_=w1_grouped[:, a * P * PACK : (a + 1) * P * PACK],
            )

        wt_codes = const.tile([P, TAPS, C], U32, align_bytes=64)
        wt_scales = const.tile([P, TAPS, C], U8, align_bytes=64)

        def quantise_and_multiply(k, up_ps, heads):
            cols = slice(heads[0] * P, (heads[-1] + 1) * P)
            nc.vector.quantize_mx(
                out=wt_codes[:, k, cols].bitcast(FP8X4),
                scales=wt_scales[:, k, cols],
                in_=wt_grouped[:, k, heads[0] : heads[-1] + 1].rearrange("p h m t -> p (h m t)"),
            )
            for h in heads:
                cols = slice(h * P, (h + 1) * P)
                nc.tensor.matmul_mx(
                    out=up_ps[:, h, :],
                    lhsT=wt_codes[:, k, cols].bitcast(FP8X4),
                    lhsT_scale=wt_scales[:, k, cols],
                    rhs=x_codes[:].bitcast(FP8X4),
                    rhs_scale=x_scales[:],
                    start=True,
                    stop=True,
                )

        up_ps_tiles = [banks.tile([P, PACK, L], F32, tag="bank", name="up_ps") for k in range(TAPS)]
        for pair in (range(0, 2), range(2, TAPS)):
            for heads in (range(PACK // 2), range(PACK // 2, PACK)):
                for k in pair:
                    quantise_and_multiply(k, up_ps_tiles[k], heads)

        keep_busy(0, UP_COLS)

        up_grouped = const.tile([P, T * PACK], BF16, align_bytes=64)
        up_codes = const.tile([P, T], U32, align_bytes=64)
        up_scales = const.tile([P, T], U8, align_bytes=64)

        def grouped_part(f):
            first, last = PARTS[f]
            part = up_grouped[:, first * TAPS * PACK : last * TAPS * PACK]
            return part.rearrange("p (k l h) -> p k l h", k=TAPS, h=PACK)

        def add_bt(f, k):
            first, last = PARTS[f]
            nc.vector.tensor_tensor(
                out=grouped_part(f)[:, k],
                in0=up_ps_tiles[k][:].rearrange("p h l -> p l h")[:, first:last, :],
                in1=bt_cols[:].unsqueeze(1).to_broadcast([P, last - first, PACK]),
                op=ADD,
            )

        def add_bt_on_scalar(k, parts):
            up_planes = planes.tile([P, PACK, L], BF16)
            first = PARTS[parts[0]][0]
            for h in range(PACK):
                nc.scalar.activation(
                    out=up_planes[:, h, first:], in_=up_ps_tiles[k][:, h, first:], func=IDENTITY, bias=bt_cols[:, h : h + 1]
                )
            for f in parts:
                first, last = PARTS[f]
                nc.scalar.copy(
                    out=grouped_part(f)[:, k], in_=up_planes[:, :, first:last].rearrange("p h l -> p l h")
                )

        def quantise_up(f):
            first, last = PARTS[f]
            cols = slice(first * TAPS, last * TAPS)
            nc.vector.quantize_mx(
                out=up_codes[:, cols].bitcast(FP8X4),
                scales=up_scales[:, cols],
                in_=up_grouped[:, first * TAPS * PACK : last * TAPS * PACK],
            )

        out_rows = out.rearrange("j b n (r s) -> (j b n) r s", r=REPEAT)

        def multiply_y(f, a):
            rows = slice(a * P, (a + 1) * P)
            first, last = PARTS[f]
            cols = slice(first * TAPS, last * TAPS)
            y_ps = banks.tile([P, (last - first) * TAPS], F32, tag="bank")
            nc.tensor.matmul_mx(
                out=y_ps[:],
                lhsT=w1_codes[:, rows].bitcast(FP8X4),
                lhsT_scale=w1_scales[:, rows],
                rhs=up_codes[:, cols].bitcast(FP8X4),
                rhs_scale=up_scales[:, cols],
                start=True,
                stop=True,
            )
            return y_ps

        y_sb_tiles = [
            results.tile([P, 1 if a == SPLIT_TILE else REPEAT, T], F32, name="y_sb", tag="y_sb_%d" % a)
            for a in range(Y_TILES)
        ]

        def add_b1(f, a, y_ps, on_vector):
            first, last = PARTS[f]
            y_in_time = y_sb_tiles[a][:, 0, first * TAPS : last * TAPS].rearrange("p (l k) -> p l k", k=TAPS)
            y_by_tap = y_ps[:].rearrange("p (k l) -> p l k", k=TAPS)
            if on_vector:
                nc.vector.tensor_scalar_add(out=y_in_time, in0=y_by_tap, scalar1=b1_cols[:, a : a + 1])
            else:
                nc.scalar.activation(out=y_in_time, in_=y_by_tap, func=IDENTITY, bias=b1_cols[:, a : a + 1])

        def store_part(f):
            steps = slice(PARTS[f][0] * TAPS, PARTS[f][1] * TAPS)
            nc.sync.dma_start(
                out=out_rows[SPLIT_TILE * P : (SPLIT_TILE + 1) * P, :, steps],
                in_=y_sb_tiles[SPLIT_TILE][:, :, steps].to_broadcast([P, REPEAT, steps.stop - steps.start]),
            )

        def store_whole(a):
            nc.sync.dma_start(
                out=out_rows[a * P : (a + 1) * P].rearrange("q r s -> q (r s)"),
                in_=y_sb_tiles[a][:].rearrange("p r s -> p (r s)"),
            )

        add_bt_on_scalar(0, (0, 1))
        for k in range(1, TAPS):
            add_bt(0, k)
            if k == 1:
                add_bt_on_scalar(1, (1,))
        quantise_w1(0)
        quantise_up(0)
        y_first = [multiply_y(0, 0)]
        add_b1(0, 0, y_first[0], False)
        store_part(0)
        for k in range(2, TAPS):
            add_bt(1, k)
            a = k - 1
            quantise_w1(a)
            y_first.append(multiply_y(0, a))
            add_b1(0, a, y_first[a], False)
        quantise_up(1)
        y_second = [multiply_y(1, a) for a in range(Y_TILES)]
        add_b1(1, 0, y_second[0], True)
        store_part(1)
        add_b1(1, 1, y_second[1], False)
        for a in range(1, Y_TILES):
            y_sb = y_sb_tiles[a]
            nc.vector.tensor_copy(out=y_sb[:, 1, :], in_=y_sb[:, 0, :])
            nc.scalar.copy(out=y_sb[:, 2, :], in_=y_sb[:, 0, :])
            nc.vector.tensor_copy(out=y_sb[:, 3, :], in_=y_sb[:, 0, :])
            store_whole(a)
            if a == 1:
                add_b1(1, 2, y_second[2], True)
